import numpy as np
import ml_dtypes


def mxq(x, axis, fmt="e4m3"):
    dtype, down = {"e4m3": (ml_dtypes.float8_e4m3fn, 7), "e5m2": (ml_dtypes.float8_e5m2, 14)}[fmt]
    v = np.moveaxis(np.asarray(x, np.float32).astype(ml_dtypes.bfloat16).astype(np.float64), axis, -1)
    blocks = v.reshape(v.shape[:-1] + (-1, 32))
    amax = np.abs(blocks).max(-1, keepdims=True)
    byte = np.maximum(np.where(amax > 0, np.frexp(amax)[1] - 1 + 127, 0) - down, 1)
    scale = np.exp2(byte - 127.0)
    codes = (blocks / scale).astype(np.float32).astype(dtype).astype(np.float64)
    return np.moveaxis((codes * scale).reshape(v.shape), -1, axis)


WIDE = False


def mx_kscale(k):
    if not WIDE:
        return np.ones(k)
    levels = np.array([10, -10, 5, -5, 0])
    if k % 512:
        return np.exp2(np.random.permutation(np.resize(levels, k // 32))).repeat(32)
    a = np.empty((k // 512, 16))
    for p in range(k // 512):
        a[p, :8] = np.random.permutation(np.resize(levels, 8))
        for g in range(8):
            far = levels[np.abs(levels - a[p, g]) >= 10]
            a[p, g + 8] = far[np.random.randint(len(far))]
    return np.exp2(a.ravel()).repeat(32)


BF16 = ml_dtypes.bfloat16


def bf(x):
    return np.asarray(x, np.float32).astype(BF16)


def f64(x):
    return np.asarray(x).astype(np.float64)


NA, NB, H = 4096, 1024, 1024


def sigmoid(v):
    return 1.0 / (1.0 + np.exp(-v))


def setup_inputs():
    s, t = mx_kscale(H), mx_kscale(H)
    return {"y_a": bf(np.random.standard_normal((NA, H)) * 0.25 / t),
            "y_b": bf(np.random.standard_normal((NB, H)) * s),
            "W": bf(np.random.standard_normal((H, H)) * 6.0 / H * t[:, None] / s[None, :]),
            "b": bf(np.random.standard_normal(H) * 5.0 / np.sqrt(H) * t)}


def reference(y_a, y_b, W, b):
    proj = (mxq(f64(y_b), 1, "e4m3") @ mxq(f64(W), 1, "e4m3").T) + f64(b)
    scores = mxq(f64(y_a), 1, "e4m3") @ mxq(proj, 1, "e4m3").T
    s = np.sum(sigmoid(scores), axis=1) / y_a.shape[1]
    return np.broadcast_to(s[:, None], y_a.shape).copy()

@@ -1,0 +1,239 @@
+from contextlib import ExitStack
+
+import concourse.mybir as mybir
+from concourse.masks import make_identity
+
+F32 = mybir.dt.float32
+BF16 = mybir.dt.bfloat16
+U32 = mybir.dt.uint32
+U8 = mybir.dt.uint8
+FP8X4 = mybir.dt.float8_e4m3fn_x4
+ACT = mybir.ActivationFunctionType
+ALU = mybir.AluOpType
+
+P = 128
+K = 1024
+UNIT = 512
+NA = 4096
+NB = 1024
+GROUPS = NA // UNIT
+WARM = 8
+
+FLOPS = 2 * NB * K * K + 2 * NA * NB * K
+
+
+def tile_miscore_t_kernel(tc, y_a, y_b, W, b, out):
+    nc = tc.nc
+    with ExitStack() as ctx:
+        ctx.enter_context(tc.manual_schedule())
+        const = ctx.enter_context(tc.tile_pool(name="const", bufs=1))
+        rawp = ctx.enter_context(tc.tile_pool(name="rawp", bufs=1))
+        grpp = ctx.enter_context(tc.tile_pool(name="grpp", bufs=3))
+        midp = ctx.enter_context(tc.tile_pool(name="midp", bufs=2))
+        keep = ctx.enter_context(tc.tile_pool(name="keep", bufs=1))
+        yacp = ctx.enter_context(tc.tile_pool(name="yacp", bufs=3))
+        outp = ctx.enter_context(tc.tile_pool(name="outp", bufs=3))
+        scrp = ctx.enter_context(tc.tile_pool(name="scrp", bufs=2))
+        psum = ctx.enter_context(tc.psum_pool(name="psum", bufs=4))
+
+        ident = const.tile([P, P], F32, name="ident")
+        make_identity(nc, ident[:])
+        b_raw = const.tile([P, 8], BF16, name="b_raw")
+        with nc.allow_non_contiguous_dma(reason="bias: 256 pieces of four elements, once"):
+            nc.scalar.dma_start(
+                out=b_raw[:].rearrange("p (a e) -> p a e", e=4),
+                in_=b.rearrange("(a p e) -> p a e", p=P, e=4),
+            )
+        bias = const.tile([P, 8], F32, name="bias")
+        warm = const.tile([P, 8], F32, name="warm")
+        nc.vector.memset(warm[:, 0:1], 0.0)
+        nc.scalar.activation(out=warm[:, 1:2], in_=warm[:, 0:1], func=ACT.Sigmoid)
+
+        zl = const.tile([P, P], BF16, name="zl")
+        zr = const.tile([P, UNIT], BF16, name="zr")
+        nc.vector.memset(zl[:], 0.0)
+        nc.vector.memset(zr[:], 0.0)
+
+        def idle_matmuls(n):
+            for i in range(n):
+                junk = psum.tile([P, UNIT], F32, name="junk", tag="mm")
+                nc.tensor.matmul(out=junk[:], lhsT=zl[:], rhs=zr[:], start=True, stop=True)
+
+        idle_matmuls(WARM)
+
+        ya_v = y_a.rearrange("(g p r) k -> g p r k", p=P, r=4)
+        yb_v = y_b.rearrange("(g p r) k -> g p r k", p=P, r=4)
+        w_v = W.rearrange("(g p r) k -> g p r k", p=P, r=4)
+
+        def load(name, halves):
+            raw = rawp.tile([P, 4 * K], BF16, name=name)
+            n = len(halves)
+            for i, src in enumerate(halves):
+                w = 4 * K // n
+                nc.sync.dma_start(
+                    out=raw[:, i * w : (i + 1) * w].rearrange("p (r k) -> p r k", k=K), in_=src
+                )
+            return raw
+
+        raw_yb = [None, None]
+        raw_w = [None, None]
+        raw_yb[0] = load("raw_yb0", [yb_v[0][:, 0:2, :], yb_v[0][:, 2:4, :]])
+        raw_w[0] = load("raw_w0", [w_v[0][:, 0:2, :], w_v[0][:, 2:4, :]])
+        raw_w[1] = load("raw_w1", [w_v[1][:, 0:2, :], w_v[1][:, 2:4, :]])
+        raw_yb[1] = load("raw_yb1", [yb_v[1][:, 0:2, :], yb_v[1][:, 2:4, :]])
+        raw_ya = [load("raw_ya%d" % g, [ya_v[g]]) for g in range(GROUPS)]
+
+        nc.vector.tensor_copy(out=bias[:], in_=b_raw[:])
+
+        def copy_on(which, dst, src):
+            if which == "S":
+                nc.scalar.copy(out=dst, in_=src)
+            else:
+                nc.vector.tensor_copy(out=dst, in_=src)
+
+        def transposes(raw, fill=False):
+            words = raw[:].bitcast(F32)
+            banks = []
+            for t in range(4):
+                xt = psum.tile([P, 4, P], F32, name="xt", tag="tp")
+                for c in range(4):
+                    lo = t * (K // 2) + (c // 2) * 2 * P + c % 2
+                    nc.tensor.transpose(xt[:, c, :], words[:, lo : lo + 2 * P - 1 : 2], ident[:])
+                banks.append(xt)
+                if fill and t % 2 == 1:
+                    idle_matmuls(1)
+            grp = grpp.tile([P, 4 * K], BF16, name="grp", align_bytes=64)
+            return banks, grp
+
+        def evacuate(which, banks, grp, t):
+            gw = grp[:].bitcast(F32).rearrange("p (g c u) -> p g c u", g=2, u=2)
+            copy_on(
+                which,
+                gw[:, :, t * P : (t + 1) * P, :],
+                banks[t][:].rearrange("p (g u) i -> p g i u", g=2),
+            )
+
+        def quantise(grp, op):
+            nc.vector.quantize_mx(out=op[0][:].bitcast(FP8X4), scales=op[1][:], in_=grp[:])
+
+        def prepare(raw, op, engines, fill=False):
+            banks, grp = transposes(raw, fill)
+            for t in range(4):
+                evacuate(engines[t], banks, grp, t)
+            quantise(grp, op)
+
+        def operand(pool, name):
+            codes = pool.tile([P, 2 * UNIT], U32, name=name + "_c", align_bytes=64)
+            scales = pool.tile([P, 2 * UNIT], U8, name=name + "_s", align_bytes=64)
+            return codes, scales
+
+        def mx_group(acc, lc, ls, m0, rc, rs):
+            for gk in range(2):
+                ml = slice(gk * UNIT + m0, gk * UNIT + m0 + P)
+                nl = slice(gk * UNIT, (gk + 1) * UNIT)
+                nc.tensor.matmul_mx(
+                    out=acc[:],
+                    lhsT=lc[:, ml].bitcast(FP8X4),
+                    lhsT_scale=ls[:, ml],
+                    rhs=rc[:, nl].bitcast(FP8X4),
+                    rhs_scale=rs[:, nl],
+                    start=(gk == 0),
+                    stop=(gk == 1),
+                )
+
+        yb_op = [operand(keep, "yb%d" % h) for h in range(2)]
+        w_op = [operand(keep, "w%d" % g) for g in range(2)]
+        pj_op = [operand(keep, "pj%d" % h) for h in range(2)]
+
+        def stage1(go, h, engines):
+            mid = midp.tile([P, 4 * UNIT], BF16, name="mid")
+            for t in range(4):
+                acc = psum.tile([P, UNIT], F32, name="acc", tag="mm")
+                mx_group(acc, w_op[go][0], w_op[go][1], t * P, yb_op[h][0], yb_op[h][1])
+                col = go * 4 + t
+                dst = mid[:, t * UNIT : (t + 1) * UNIT]
+                if engines[t] == "S":
+                    nc.scalar.activation(
+                        out=dst, in_=acc[:], func=ACT.Identity, bias=bias[:, col : col + 1], scale=1.0
+                    )
+                else:
+                    nc.vector.tensor_scalar(
+                        out=dst, in0=acc[:], scalar1=bias[:, col : col + 1], scalar2=None, op0=ALU.add
+                    )
+            pgrp = midp.tile([P, 4 * UNIT], BF16, name="pgrp", align_bytes=64)
+            nc.vector.tensor_copy(
+                out=pgrp[:].rearrange("p (c i t) -> p c t i", i=4, t=4),
+                in_=mid[:].rearrange("p (t c i) -> p c t i", t=4, i=4),
+            )
+            nl = slice(go * UNIT, (go + 1) * UNIT)
+            nc.vector.quantize_mx(
+                out=pj_op[h][0][:, nl].bitcast(FP8X4), scales=pj_op[h][1][:, nl], in_=pgrp[:]
+            )
+
+        out_v = out.rearrange("(g p r) (c k) -> g c p r k", p=P, r=4, c=2)
+
+        def scores(g, op, sums, r, h):
+            acc = psum.tile([P, UNIT], F32, name="acc", tag="mm")
+            mx_group(acc, op[0], op[1], r * P, pj_op[h][0], pj_op[h][1])
+            scr = scrp.tile([P, UNIT], F32, name="scr")
+            col = 2 * r + h
+            nc.scalar.activation(
+                out=scr[:], in_=acc[:], func=ACT.Sigmoid, accum_out=sums[:, col : col + 1]
+            )
+
+        def finish(g, sums, ot, r):
+            filler = nc.vector if g == GROUPS - 1 else nc.gpsimd
+            filler.tensor_scalar(
+                out=ot[:, r * UNIT : (r + 1) * UNIT],
+                in0=sums[:, 2 * r : 2 * r + 1].to_broadcast([P, UNIT]),
+                scalar1=sums[:, 2 * r + 1 : 2 * r + 2],
+                scalar2=1.0 / K,
+                op0=ALU.add,
+                op1=ALU.mult,
+            )
+            for c in range(2):
+                nc.sync.dma_start(out=out_v[g][c][:, r, :], in_=ot[:, r * UNIT : (r + 1) * UNIT])
+
+        prepare(raw_yb[0], yb_op[0], "SVSS", True)
+        prepare(raw_w[0], w_op[0], "SVSS", True)
+        prepare(raw_w[1], w_op[1], "SVSS", True)
+        stage1(0, 0, "SSSS")
+        prepare(raw_yb[1], yb_op[1], "SVSS")
+        stage1(1, 0, "SSSS")
+        ya_op = operand(yacp, "ya")
+        prepare(raw_ya[0], ya_op, "SVSV")
+        stage1(0, 1, "SSSS")
+        stage1(1, 1, "SSSS")
+        late = None
+        for g in range(GROUPS):
+            sums = scrp.tile([P, 8], F32, name="sums", bufs=3)
+            ot = outp.tile([P, 4 * UNIT], F32, name="ot")
+            more = g + 1 < GROUPS
+            if more:
+                next_op = operand(yacp, "ya")
+                banks, grp = transposes(raw_ya[g + 1])
+                evacuate("V", banks, grp, 0)
+            if late is not None:
+                finish(*late)
+            if more:
+                for t in range(1, 4):
+                    evacuate("V", banks, grp, t)
+            if g == 0:
+                for h in range(2):
+                    for r in range(4):
+                        scores(g, ya_op, sums, r, h)
+                quantise(grp, next_op)
+                for r in range(3):
+                    finish(g, sums, ot, r)
+            else:
+                for r in range(4):
+                    for h in range(2):
+                        scores(g, ya_op, sums, r, h)
+                    if r < 3:
+                        finish(g, sums, ot, r)
+                    if r == 0 and more:
+                        quantise(grp, next_op)
+            late = (g, sums, ot, 3)
+            if more:
+                ya_op = next_op
+        finish(*late)

@@ -28,6 +28,7 @@ def tile_miscore_t_kernel(tc, y_a, y_b, W, b, out):
         ctx.enter_context(tc.manual_schedule())
         const = ctx.enter_context(tc.tile_pool(name="const", bufs=1))
         rawp = ctx.enter_context(tc.tile_pool(name="rawp", bufs=1))
+        sortp = ctx.enter_context(tc.tile_pool(name="sortp", bufs=2))
         grpp = ctx.enter_context(tc.tile_pool(name="grpp", bufs=3))
         midp = ctx.enter_context(tc.tile_pool(name="midp", bufs=2))
         keep = ctx.enter_context(tc.tile_pool(name="keep", bufs=1))
@@ -91,14 +92,27 @@ def tile_miscore_t_kernel(tc, y_a, y_b, W, b, out):
             else:
                 nc.vector.tensor_copy(out=dst, in_=src)
 
-        def transposes(raw, fill=False):
+        def sort_words(raw):
+            tile = sortp.tile([P, 4 * K], BF16, name="sorted")
+            nc.vector.tensor_copy(
+                out=tile[:].bitcast(F32).rearrange("p (a u i) -> p a u i", u=2, i=P),
+                in_=raw[:].bitcast(F32).rearrange("p (a i u) -> p a u i", u=2, i=P),
+            )
+            return tile
+
+        def transposes(raw, fill=False, in_order=False):
             words = raw[:].bitcast(F32)
             banks = []
             for t in range(4):
                 xt = psum.tile([P, 4, P], F32, name="xt", tag="tp")
                 for c in range(4):
-                    lo = t * (K // 2) + (c // 2) * 2 * P + c % 2
-                    nc.tensor.transpose(xt[:, c, :], words[:, lo : lo + 2 * P - 1 : 2], ident[:])
+                    if in_order:
+                        lo = t * (K // 2) + c * P
+                        part = words[:, lo : lo + P]
+                    else:
+                        lo = t * (K // 2) + (c // 2) * 2 * P + c % 2
+                        part = words[:, lo : lo + 2 * P - 1 : 2]
+                    nc.tensor.transpose(xt[:, c, :], part, ident[:])
                 banks.append(xt)
                 if fill and t % 2 == 1:
                     idle_matmuls(1)
@@ -116,8 +130,8 @@ def tile_miscore_t_kernel(tc, y_a, y_b, W, b, out):
         def quantise(grp, op):
             nc.vector.quantize_mx(out=op[0][:].bitcast(FP8X4), scales=op[1][:], in_=grp[:])
 
-        def prepare(raw, op, engines, fill=False):
-            banks, grp = transposes(raw, fill)
+        def prepare(raw, op, engines, fill=False, in_order=False):
+            banks, grp = transposes(raw, fill, in_order)
             for t in range(4):
                 evacuate(engines[t], banks, grp, t)
             quantise(grp, op)
@@ -199,10 +213,12 @@ def tile_miscore_t_kernel(tc, y_a, y_b, W, b, out):
         prepare(raw_w[1], w_op[1], "SVSS", True)
         stage1(0, 0, "SSSS")
         prepare(raw_yb[1], yb_op[1], "SVSS")
+        ya_sorted = sort_words(raw_ya[0])
         stage1(1, 0, "SSSS")
         ya_op = operand(yacp, "ya")
-        prepare(raw_ya[0], ya_op, "SVSV")
+        prepare(ya_sorted, ya_op, "SVSV", False, True)
         stage1(0, 1, "SSSS")
+        ya_sorted = sort_words(raw_ya[1])
         stage1(1, 1, "SSSS")
         late = None
         for g in range(GROUPS):
@@ -211,13 +227,15 @@ def tile_miscore_t_kernel(tc, y_a, y_b, W, b, out):
             more = g + 1 < GROUPS
             if more:
                 next_op = operand(yacp, "ya")
-                banks, grp = transposes(raw_ya[g + 1])
+                banks, grp = transposes(ya_sorted, False, True)
                 evacuate("V", banks, grp, 0)
             if late is not None:
                 finish(*late)
             if more:
                 for t in range(1, 4):
                     evacuate("V", banks, grp, t)
+            if g + 2 < GROUPS:
+                ya_sorted = sort_words(raw_ya[g + 2])
             if g == 0:
                 for h in range(2):
                     for r in range(4):

@@ -17,7 +17,7 @@ UNIT = 512
 NA = 4096
 NB = 1024
 GROUPS = NA // UNIT
-WARM = 8
+WARM = 4
 
 FLOPS = 2 * NB * K * K + 2 * NA * NB * K
 
@@ -27,8 +27,8 @@ def tile_miscore_t_kernel(tc, y_a, y_b, W, b, out):
     with ExitStack() as ctx:
         ctx.enter_context(tc.manual_schedule())
         const = ctx.enter_context(tc.tile_pool(name="const", bufs=1))
-        rawp = ctx.enter_context(tc.tile_pool(name="rawp", bufs=1))
-        sortp = ctx.enter_context(tc.tile_pool(name="sortp", bufs=2))
+        rawp = ctx.enter_context(tc.tile_pool(name="rawp", bufs=8))
+        sortp = ctx.enter_context(tc.tile_pool(name="sortp", bufs=3))
         grpp = ctx.enter_context(tc.tile_pool(name="grpp", bufs=3))
         midp = ctx.enter_context(tc.tile_pool(name="midp", bufs=2))
         keep = ctx.enter_context(tc.tile_pool(name="keep", bufs=1))
@@ -37,23 +37,22 @@ def tile_miscore_t_kernel(tc, y_a, y_b, W, b, out):
         scrp = ctx.enter_context(tc.tile_pool(name="scrp", bufs=2))
         psum = ctx.enter_context(tc.psum_pool(name="psum", bufs=4))
 
+        zl = const.tile([P, P], BF16, name="zl")
+        zr = const.tile([P, UNIT], BF16, name="zr")
+        nc.vector.memset(zl[:], 0.0)
+        nc.vector.memset(zr[:], 0.0)
         ident = const.tile([P, P], F32, name="ident")
         make_identity(nc, ident[:])
         b_raw = const.tile([P, 8], BF16, name="b_raw")
         with nc.allow_non_contiguous_dma(reason="bias: 256 pieces of four elements, once"):
             nc.scalar.dma_start(
-                out=b_raw[:].rearrange("p (a e) -> p a e", e=4),
-                in_=b.rearrange("(a p e) -> p a e", p=P, e=4),
+                out=b_raw[:].rearrange("p (a t) -> p a t", t=4),
+                in_=b.rearrange("(a p t) -> p a t", p=P, t=4),
             )
         bias = const.tile([P, 8], F32, name="bias")
         warm = const.tile([P, 8], F32, name="warm")
         nc.vector.memset(warm[:, 0:1], 0.0)
         nc.scalar.activation(out=warm[:, 1:2], in_=warm[:, 0:1], func=ACT.Sigmoid)
-
-        zl = const.tile([P, P], BF16, name="zl")
-        zr = const.tile([P, UNIT], BF16, name="zr")
-        nc.vector.memset(zl[:], 0.0)
-        nc.vector.memset(zr[:], 0.0)
 
         def idle_matmuls(n):
             for i in range(n):
@@ -62,29 +61,30 @@ def tile_miscore_t_kernel(tc, y_a, y_b, W, b, out):
 
         idle_matmuls(WARM)
 
-        ya_v = y_a.rearrange("(g p r) k -> g p r k", p=P, r=4)
-        yb_v = y_b.rearrange("(g p r) k -> g p r k", p=P, r=4)
-        w_v = W.rearrange("(g p r) k -> g p r k", p=P, r=4)
+        def rows_of(x):
+            return x.rearrange("(g p r) k -> g p r k", p=P, r=4)
 
-        def load(name, halves):
-            raw = rawp.tile([P, 4 * K], BF16, name=name)
-            n = len(halves)
-            for i, src in enumerate(halves):
-                w = 4 * K // n
+        def load(src, pieces):
+            raw = rawp.tile([P, 4 * K], BF16, name="raw")
+            n = 4 // pieces
+            for i in range(pieces):
                 nc.sync.dma_start(
-                    out=raw[:, i * w : (i + 1) * w].rearrange("p (r k) -> p r k", k=K), in_=src
+                    out=raw[:, i * n * K : (i + 1) * n * K].rearrange("p (r k) -> p r k", k=K),
+                    in_=src[:, i * n : (i + 1) * n, :],
                 )
             return raw
 
         raw_yb = [None, None]
         raw_w = [None, None]
-        raw_yb[0] = load("raw_yb0", [yb_v[0][:, 0:2, :], yb_v[0][:, 2:4, :]])
-        raw_w[0] = load("raw_w0", [w_v[0][:, 0:2, :], w_v[0][:, 2:4, :]])
-        raw_w[1] = load("raw_w1", [w_v[1][:, 0:2, :], w_v[1][:, 2:4, :]])
-        raw_yb[1] = load("raw_yb1", [yb_v[1][:, 0:2, :], yb_v[1][:, 2:4, :]])
-        raw_ya = [load("raw_ya%d" % g, [ya_v[g]]) for g in range(GROUPS)]
+        raw_yb[0] = load(rows_of(y_b)[0], 2)
+        raw_w[0] = load(rows_of(W)[0], 2)
+        raw_w[1] = load(rows_of(W)[1], 2)
+        raw_yb[1] = load(rows_of(y_b)[1], 2)
 
-        nc.vector.tensor_copy(out=bias[:], in_=b_raw[:])
+        def load_ya(g):
+            return load(rows_of(y_a)[g], 1)
+
+        raw_ya = [load_ya(g) for g in range(4)]
 
         def copy_on(which, dst, src):
             if which == "S":
@@ -92,49 +92,50 @@ def tile_miscore_t_kernel(tc, y_a, y_b, W, b, out):
             else:
                 nc.vector.tensor_copy(out=dst, in_=src)
 
-        def sort_words(raw):
-            tile = sortp.tile([P, 4 * K], BF16, name="sorted")
-            nc.vector.tensor_copy(
-                out=tile[:].bitcast(F32).rearrange("p (a u i) -> p a u i", u=2, i=P),
-                in_=raw[:].bitcast(F32).rearrange("p (a i u) -> p a u i", u=2, i=P),
+        def new_sorted():
+            return sortp.tile([P, 4 * K], BF16, name="sorted")
+
+        def sort_words(tile, raw, r0, r1, which="V"):
+            cols = slice(r0 * K, r1 * K)
+            copy_on(
+                which,
+                tile[:, cols].bitcast(F32).rearrange("p (a u i) -> p a u i", u=2, i=P),
+                raw[:, cols].bitcast(F32).rearrange("p (a i u) -> p a u i", u=2, i=P),
             )
+
+        def sorted_copy(raw):
+            tile = new_sorted()
+            sort_words(tile, raw, 0, 4)
             return tile
 
-        def transposes(raw, fill=False, in_order=False):
-            words = raw[:].bitcast(F32)
-            banks = []
-            for t in range(4):
-                xt = psum.tile([P, 4, P], F32, name="xt", tag="tp")
-                for c in range(4):
-                    if in_order:
-                        lo = t * (K // 2) + c * P
-                        part = words[:, lo : lo + P]
-                    else:
-                        lo = t * (K // 2) + (c // 2) * 2 * P + c % 2
-                        part = words[:, lo : lo + 2 * P - 1 : 2]
-                    nc.tensor.transpose(xt[:, c, :], part, ident[:])
-                banks.append(xt)
-                if fill and t % 2 == 1:
-                    idle_matmuls(1)
-            grp = grpp.tile([P, 4 * K], BF16, name="grp", align_bytes=64)
-            return banks, grp
+        def transpose_rows(tile, t):
+            words = tile[:].bitcast(F32)
+            xt = psum.tile([P, 4, P], F32, name="xt", tag="tp")
+            for c in range(4):
+                lo = t * (K // 2) + c * P
+                nc.tensor.transpose(xt[:, c, :], words[:, lo : lo + P], ident[:])
+            return xt
 
-        def evacuate(which, banks, grp, t):
+        def new_grouped():
+            return grpp.tile([P, 4 * K], BF16, name="grp", align_bytes=64)
+
+        def evacuate(which, bank, grp, t):
             gw = grp[:].bitcast(F32).rearrange("p (g c u) -> p g c u", g=2, u=2)
             copy_on(
                 which,
                 gw[:, :, t * P : (t + 1) * P, :],
-                banks[t][:].rearrange("p (g u) i -> p g i u", g=2),
+                bank[:].rearrange("p (g u) i -> p g i u", g=2),
             )
 
         def quantise(grp, op):
             nc.vector.quantize_mx(out=op[0][:].bitcast(FP8X4), scales=op[1][:], in_=grp[:])
 
-        def prepare(raw, op, engines, fill=False, in_order=False):
-            banks, grp = transposes(raw, fill, in_order)
+        def transpose_unit(tile, engines):
+            grp = new_grouped()
+            banks = [transpose_rows(tile, t) for t in range(4)]
             for t in range(4):
-                evacuate(engines[t], banks, grp, t)
-            quantise(grp, op)
+                evacuate(engines[t], banks[t], grp, t)
+            return grp
 
         def operand(pool, name):
             codes = pool.tile([P, 2 * UNIT], U32, name=name + "_c", align_bytes=64)
@@ -159,7 +160,7 @@ def tile_miscore_t_kernel(tc, y_a, y_b, W, b, out):
         w_op = [operand(keep, "w%d" % g) for g in range(2)]
         pj_op = [operand(keep, "pj%d" % h) for h in range(2)]
 
-        def stage1(go, h, engines):
+        def project(go, h, engines="SSSS"):
             mid = midp.tile([P, 4 * UNIT], BF16, name="mid")
             for t in range(4):
                 acc = psum.tile([P, UNIT], F32, name="acc", tag="mm")
@@ -174,11 +175,17 @@ def tile_miscore_t_kernel(tc, y_a, y_b, W, b, out):
                     nc.vector.tensor_scalar(
                         out=dst, in0=acc[:], scalar1=bias[:, col : col + 1], scalar2=None, op0=ALU.add
                     )
+            return mid
+
+        def regroup(mid):
             pgrp = midp.tile([P, 4 * UNIT], BF16, name="pgrp", align_bytes=64)
             nc.vector.tensor_copy(
                 out=pgrp[:].rearrange("p (c i t) -> p c t i", i=4, t=4),
                 in_=mid[:].rearrange("p (t c i) -> p c t i", t=4, i=4),
             )
+            return pgrp
+
+        def quantise_proj(go, h, pgrp):
             nl = slice(go * UNIT, (go + 1) * UNIT)
             nc.vector.quantize_mx(
                 out=pj_op[h][0][:, nl].bitcast(FP8X4), scales=pj_op[h][1][:, nl], in_=pgrp[:]
@@ -208,18 +215,43 @@ def tile_miscore_t_kernel(tc, y_a, y_b, W, b, out):
             for c in range(2):
                 nc.sync.dma_start(out=out_v[g][c][:, r, :], in_=ot[:, r * UNIT : (r + 1) * UNIT])
 
-        prepare(raw_yb[0], yb_op[0], "SVSS", True)
-        prepare(raw_w[0], w_op[0], "SVSS", True)
-        prepare(raw_w[1], w_op[1], "SVSS", True)
-        stage1(0, 0, "SSSS")
-        prepare(raw_yb[1], yb_op[1], "SVSS")
-        ya_sorted = sort_words(raw_ya[0])
-        stage1(1, 0, "SSSS")
+        def sort_halves(raw):
+            tile = new_sorted()
+            sort_words(tile, raw, 0, 2)
+            sort_words(tile, raw, 2, 4)
+            return tile
+
+        s_yb0 = sort_halves(raw_yb[0])
+        nc.vector.tensor_copy(out=bias[:], in_=b_raw[:])
+        s_w0 = sort_halves(raw_w[0])
+        g_yb0 = transpose_unit(s_yb0, "SSSS")
+        quantise(g_yb0, yb_op[0])
+        s_w1 = sort_halves(raw_w[1])
+        g_w0 = transpose_unit(s_w0, "SSSS")
+        quantise(g_w0, w_op[0])
+        s_yb1 = sort_halves(raw_yb[1])
+        g_w1 = transpose_unit(s_w1, "SSSS")
+        quantise(g_w1, w_op[1])
+        mid00 = project(0, 0)
+        s_ya = sorted_copy(raw_ya[0])
+        raw_ya.append(load_ya(4))
+        g_yb1 = transpose_unit(s_yb1, "VSVS")
+        quantise(g_yb1, yb_op[1])
+        p00 = regroup(mid00)
+        mid10 = project(1, 0)
+        quantise_proj(0, 0, p00)
+        s_next = sorted_copy(raw_ya[1])
+        raw_ya.append(load_ya(5))
+        p10 = regroup(mid10)
+        g_ya = transpose_unit(s_ya, "VVVV")
+        quantise_proj(1, 0, p10)
+        mid01 = project(0, 1)
         ya_op = operand(yacp, "ya")
-        prepare(ya_sorted, ya_op, "SVSV", False, True)
-        stage1(0, 1, "SSSS")
-        ya_sorted = sort_words(raw_ya[1])
-        stage1(1, 1, "SSSS")
+        quantise(g_ya, ya_op)
+        p01 = regroup(mid01)
+        mid11 = project(1, 1)
+        raw_ya.append(load_ya(6))
+        raw_ya.append(load_ya(7))
         late = None
         for g in range(GROUPS):
             sums = scrp.tile([P, 8], F32, name="sums", bufs=3)
@@ -227,23 +259,31 @@ def tile_miscore_t_kernel(tc, y_a, y_b, W, b, out):
             more = g + 1 < GROUPS
             if more:
                 next_op = operand(yacp, "ya")
-                banks, grp = transposes(ya_sorted, False, True)
-                evacuate("V", banks, grp, 0)
+                banks = [transpose_rows(s_next, t) for t in range(4)]
+                grp = new_grouped()
+                if g == 0:
+                    quantise_proj(0, 1, p01)
+                    p11 = regroup(mid11)
+                evacuate("V", banks[0], grp, 0)
+                if g == 0:
+                    quantise_proj(1, 1, p11)
             if late is not None:
                 finish(*late)
             if more:
                 for t in range(1, 4):
-                    evacuate("V", banks, grp, t)
-            if g + 2 < GROUPS:
-                ya_sorted = sort_words(raw_ya[g + 2])
+                    evacuate("V", banks[t], grp, t)
             if g == 0:
-                for h in range(2):
-                    for r in range(4):
-                        scores(g, ya_op, sums, r, h)
+                for r in range(4):
+                    scores(g, ya_op, sums, r, 0)
+                s_next = sorted_copy(raw_ya[g + 2])
+                for r in range(4):
+                    scores(g, ya_op, sums, r, 1)
                 quantise(grp, next_op)
                 for r in range(3):
                     finish(g, sums, ot, r)
             else:
+                if g + 2 < GROUPS:
+                    s_next = sorted_copy(raw_ya[g + 2])
                 for r in range(4):
                     for h in range(2):
                         scores(g, ya_op, sums, r, h)

@@ -17,6 +17,7 @@ UNIT = 512
 NA = 4096
 NB = 1024
 GROUPS = NA // UNIT
+FILL = 256
 WARM = 4
 
 FLOPS = 2 * NB * K * K + 2 * NA * NB * K
@@ -191,7 +192,7 @@ def tile_miscore_t_kernel(tc, y_a, y_b, W, b, out):
                 out=pj_op[h][0][:, nl].bitcast(FP8X4), scales=pj_op[h][1][:, nl], in_=pgrp[:]
             )
 
-        out_v = out.rearrange("(g p r) (c k) -> g c p r k", p=P, r=4, c=2)
+        out_v = out.rearrange("(g p r) (c k) -> g p r c k", p=P, r=4, k=FILL)
 
         def scores(g, op, sums, r, h):
             acc = psum.tile([P, UNIT], F32, name="acc", tag="mm")
@@ -203,17 +204,18 @@ def tile_miscore_t_kernel(tc, y_a, y_b, W, b, out):
             )
 
         def finish(g, sums, ot, r):
-            filler = nc.vector if g == GROUPS - 1 else nc.gpsimd
-            filler.tensor_scalar(
-                out=ot[:, r * UNIT : (r + 1) * UNIT],
-                in0=sums[:, 2 * r : 2 * r + 1].to_broadcast([P, UNIT]),
+            nc.vector.tensor_scalar(
+                out=ot[:, r * FILL : (r + 1) * FILL],
+                in0=sums[:, 2 * r : 2 * r + 1].to_broadcast([P, FILL]),
                 scalar1=sums[:, 2 * r + 1 : 2 * r + 2],
                 scalar2=1.0 / K,
                 op0=ALU.add,
                 op1=ALU.mult,
             )
-            for c in range(2):
-                nc.sync.dma_start(out=out_v[g][c][:, r, :], in_=ot[:, r * UNIT : (r + 1) * UNIT])
+            nc.sync.dma_start(
+                out=out_v[g][:, r, :, :],
+                in_=ot[:, r * FILL : (r + 1) * FILL].unsqueeze(1).to_broadcast([P, K // FILL, FILL]),
+            )
 
         def sort_halves(raw):
             tile = new_sorted()
@@ -243,7 +245,7 @@ def tile_miscore_t_kernel(tc, y_a, y_b, W, b, out):
         s_next = sorted_copy(raw_ya[1])
         raw_ya.append(load_ya(5))
         p10 = regroup(mid10)
-        g_ya = transpose_unit(s_ya, "VVVV")
+        g_ya = transpose_unit(s_ya, "SVSV")
         quantise_proj(1, 0, p10)
         mid01 = project(0, 1)
         ya_op = operand(yacp, "ya")
@@ -255,7 +257,7 @@ def tile_miscore_t_kernel(tc, y_a, y_b, W, b, out):
         late = None
         for g in range(GROUPS):
             sums = scrp.tile([P, 8], F32, name="sums", bufs=3)
-            ot = outp.tile([P, 4 * UNIT], F32, name="ot")
+            ot = outp.tile([P, 4 * FILL], F32, name="ot")
             more = g + 1 < GROUPS
             if more:
                 next_op = operand(yacp, "ya")

@@ -17,7 +17,7 @@ UNIT = 512
 NA = 4096
 NB = 1024
 GROUPS = NA // UNIT
-FILL = 256
+FILL = 512
 WARM = 4
 
 FLOPS = 2 * NB * K * K + 2 * NA * NB * K
@@ -267,12 +267,13 @@ def tile_miscore_t_kernel(tc, y_a, y_b, W, b, out):
                     quantise_proj(0, 1, p01)
                     p11 = regroup(mid11)
                 evacuate("V", banks[0], grp, 0)
+                evacuate("S", banks[3], grp, 3)
                 if g == 0:
                     quantise_proj(1, 1, p11)
             if late is not None:
                 finish(*late)
             if more:
-                for t in range(1, 4):
+                for t in range(1, 3):
                     evacuate("V", banks[t], grp, t)
             if g == 0:
                 for r in range(4):
@@ -280,9 +281,10 @@ def tile_miscore_t_kernel(tc, y_a, y_b, W, b, out):
                 s_next = sorted_copy(raw_ya[g + 2])
                 for r in range(4):
                     scores(g, ya_op, sums, r, 1)
-                quantise(grp, next_op)
-                for r in range(3):
-                    finish(g, sums, ot, r)
+                    if r < 3:
+                        finish(g, sums, ot, r)
+                    if r == 0:
+                        quantise(grp, next_op)
             else:
                 if g + 2 < GROUPS:
                     s_next = sorted_copy(raw_ya[g + 2])

@@ -31,7 +31,7 @@ def tile_miscore_t_kernel(tc, y_a, y_b, W, b, out):
         rawp = ctx.enter_context(tc.tile_pool(name="rawp", bufs=8))
         sortp = ctx.enter_context(tc.tile_pool(name="sortp", bufs=3))
         grpp = ctx.enter_context(tc.tile_pool(name="grpp", bufs=3))
-        midp = ctx.enter_context(tc.tile_pool(name="midp", bufs=2))
+        midp = ctx.enter_context(tc.tile_pool(name="midp", bufs=3))
         keep = ctx.enter_context(tc.tile_pool(name="keep", bufs=1))
         yacp = ctx.enter_context(tc.tile_pool(name="yacp", bufs=3))
         outp = ctx.enter_context(tc.tile_pool(name="outp", bufs=3))
@@ -104,17 +104,24 @@ def tile_miscore_t_kernel(tc, y_a, y_b, W, b, out):
                 raw[:, cols].bitcast(F32).rearrange("p (a i u) -> p a u i", u=2, i=P),
             )
 
-        def sorted_copy(raw):
+        def sorted_copy(raw, pieces=0):
             tile = new_sorted()
-            sort_words(tile, raw, 0, 4)
+            if pieces == 0:
+                sort_words(tile, raw, 0, 4)
+            for i in range(pieces):
+                cols = slice(i * 4 * K // pieces, (i + 1) * 4 * K // pieces)
+                nc.gpsimd.tensor_copy(
+                    out=tile[:, cols].bitcast(U32).rearrange("p (a u i) -> p a u i", u=2, i=P),
+                    in_=raw[:, cols].bitcast(U32).rearrange("p (a i u) -> p a u i", u=2, i=P),
+                )
             return tile
 
-        def transpose_rows(tile, t):
+        def transpose_rows(tile, t, step=1):
             words = tile[:].bitcast(F32)
             xt = psum.tile([P, 4, P], F32, name="xt", tag="tp")
             for c in range(4):
-                lo = t * (K // 2) + c * P
-                nc.tensor.transpose(xt[:, c, :], words[:, lo : lo + P], ident[:])
+                lo = t * (K // 2) + (c * P if step == 1 else (c // 2) * 2 * P + c % 2)
+                nc.tensor.transpose(xt[:, c, :], words[:, lo : lo + step * (P - 1) + 1 : step], ident[:])
             return xt
 
         def new_grouped():
@@ -131,9 +138,9 @@ def tile_miscore_t_kernel(tc, y_a, y_b, W, b, out):
         def quantise(grp, op):
             nc.vector.quantize_mx(out=op[0][:].bitcast(FP8X4), scales=op[1][:], in_=grp[:])
 
-        def transpose_unit(tile, engines):
+        def transpose_unit(tile, engines, step=1):
             grp = new_grouped()
-            banks = [transpose_rows(tile, t) for t in range(4)]
+            banks = [transpose_rows(tile, t, step) for t in range(4)]
             for t in range(4):
                 evacuate(engines[t], banks[t], grp, t)
             return grp
@@ -223,33 +230,32 @@ def tile_miscore_t_kernel(tc, y_a, y_b, W, b, out):
             sort_words(tile, raw, 2, 4)
             return tile
 
-        s_yb0 = sort_halves(raw_yb[0])
         nc.vector.tensor_copy(out=bias[:], in_=b_raw[:])
-        s_w0 = sort_halves(raw_w[0])
-        g_yb0 = transpose_unit(s_yb0, "SSSS")
+        g_yb0 = transpose_unit(raw_yb[0], "SVSV", 2)
+        g_w0 = transpose_unit(raw_w[0], "SSSS", 2)
         quantise(g_yb0, yb_op[0])
+        idle_matmuls(2)
         s_w1 = sort_halves(raw_w[1])
-        g_w0 = transpose_unit(s_w0, "SSSS")
         quantise(g_w0, w_op[0])
-        s_yb1 = sort_halves(raw_yb[1])
         g_w1 = transpose_unit(s_w1, "SSSS")
-        quantise(g_w1, w_op[1])
+        s_yb1 = sort_halves(raw_yb[1])
         mid00 = project(0, 0)
+        quantise(g_w1, w_op[1])
+        g_yb1 = transpose_unit(s_yb1, "VSVS")
         s_ya = sorted_copy(raw_ya[0])
         raw_ya.append(load_ya(4))
-        g_yb1 = transpose_unit(s_yb1, "VSVS")
         quantise(g_yb1, yb_op[1])
         p00 = regroup(mid00)
         mid10 = project(1, 0)
         quantise_proj(0, 0, p00)
-        s_next = sorted_copy(raw_ya[1])
+        s_next = sorted_copy(raw_ya[1], 4)
         raw_ya.append(load_ya(5))
-        p10 = regroup(mid10)
         g_ya = transpose_unit(s_ya, "SVSV")
-        quantise_proj(1, 0, p10)
+        p10 = regroup(mid10)
         mid01 = project(0, 1)
         ya_op = operand(yacp, "ya")
         quantise(g_ya, ya_op)
+        quantise_proj(1, 0, p10)
         p01 = regroup(mid01)
         mid11 = project(1, 1)
         raw_ya.append(load_ya(6))
@@ -278,7 +284,7 @@ def tile_miscore_t_kernel(tc, y_a, y_b, W, b, out):
             if g == 0:
                 for r in range(4):
                     scores(g, ya_op, sums, r, 0)
-                s_next = sorted_copy(raw_ya[g + 2])
+                s_next = sorted_copy(raw_ya[g + 2], 4)
                 for r in range(4):
                     scores(g, ya_op, sums, r, 1)
                     if r < 3:
@@ -287,7 +293,7 @@ def tile_miscore_t_kernel(tc, y_a, y_b, W, b, out):
                         quantise(grp, next_op)
             else:
                 if g + 2 < GROUPS:
-                    s_next = sorted_copy(raw_ya[g + 2])
+                    s_next = sorted_copy(raw_ya[g + 2], 4)
                 for r in range(4):
                     for h in range(2):
                         scores(g, ya_op, sums, r, h)

@@ -138,9 +138,13 @@ def tile_miscore_t_kernel(tc, y_a, y_b, W, b, out):
         def quantise(grp, op):
             nc.vector.quantize_mx(out=op[0][:].bitcast(FP8X4), scales=op[1][:], in_=grp[:])
 
-        def transpose_unit(tile, engines, step=1):
+        def transpose_unit(tile, engines, step=1, fill=False):
             grp = new_grouped()
-            banks = [transpose_rows(tile, t, step) for t in range(4)]
+            banks = []
+            for t in range(4):
+                banks.append(transpose_rows(tile, t, step))
+                if fill and t % 2 == 1:
+                    idle_matmuls(1)
             for t in range(4):
                 evacuate(engines[t], banks[t], grp, t)
             return grp
@@ -231,26 +235,24 @@ def tile_miscore_t_kernel(tc, y_a, y_b, W, b, out):
             return tile
 
         nc.vector.tensor_copy(out=bias[:], in_=b_raw[:])
-        g_yb0 = transpose_unit(raw_yb[0], "SVSV", 2)
-        g_w0 = transpose_unit(raw_w[0], "SSSS", 2)
+        g_yb0 = transpose_unit(raw_yb[0], "SVSV", 2, True)
+        g_w0 = transpose_unit(raw_w[0], "SSSS", 2, True)
         quantise(g_yb0, yb_op[0])
-        idle_matmuls(2)
-        s_w1 = sort_halves(raw_w[1])
         quantise(g_w0, w_op[0])
-        g_w1 = transpose_unit(s_w1, "SSSS")
-        s_yb1 = sort_halves(raw_yb[1])
+        g_w1 = transpose_unit(raw_w[1], "SSVS", 2, True)
+        s_yb1 = new_sorted()
+        sort_words(s_yb1, raw_yb[1], 0, 2)
         mid00 = project(0, 0)
         quantise(g_w1, w_op[1])
+        sort_words(s_yb1, raw_yb[1], 2, 4)
         g_yb1 = transpose_unit(s_yb1, "VSVS")
-        s_ya = sorted_copy(raw_ya[0])
         raw_ya.append(load_ya(4))
         quantise(g_yb1, yb_op[1])
         p00 = regroup(mid00)
         mid10 = project(1, 0)
         quantise_proj(0, 0, p00)
-        s_next = sorted_copy(raw_ya[1], 4)
         raw_ya.append(load_ya(5))
-        g_ya = transpose_unit(s_ya, "SVSV")
+        g_ya = transpose_unit(raw_ya[0], "SVSV", 2)
         p10 = regroup(mid10)
         mid01 = project(0, 1)
         ya_op = operand(yacp, "ya")
@@ -267,7 +269,7 @@ def tile_miscore_t_kernel(tc, y_a, y_b, W, b, out):
             more = g + 1 < GROUPS
             if more:
                 next_op = operand(yacp, "ya")
-                banks = [transpose_rows(s_next, t) for t in range(4)]
+                banks = [transpose_rows(raw_ya[1], t, 2) if g == 0 else transpose_rows(s_next, t) for t in range(4)]
                 grp = new_grouped()
                 if g == 0:
                     quantise_proj(0, 1, p01)
@@ -284,7 +286,7 @@ def tile_miscore_t_kernel(tc, y_a, y_b, W, b, out):
             if g == 0:
                 for r in range(4):
                     scores(g, ya_op, sums, r, 0)
-                s_next = sorted_copy(raw_ya[g + 2], 4)
+                s_next = sorted_copy(raw_ya[g + 2])
                 for r in range(4):
                     scores(g, ya_op, sums, r, 1)
                     if r < 3:
@@ -293,7 +295,7 @@ def tile_miscore_t_kernel(tc, y_a, y_b, W, b, out):
                         quantise(grp, next_op)
             else:
                 if g + 2 < GROUPS:
-                    s_next = sorted_copy(raw_ya[g + 2], 4)
+                    s_next = sorted_copy(raw_ya[g + 2])
                 for r in range(4):
                     for h in range(2):
                         scores(g, ya_op, sums, r, h)

from contextlib import ExitStack

import concourse.mybir as mybir
from concourse.masks import make_identity

F32 = mybir.dt.float32
BF16 = mybir.dt.bfloat16
U32 = mybir.dt.uint32
U8 = mybir.dt.uint8
FP8X4 = mybir.dt.float8_e4m3fn_x4
ACT = mybir.ActivationFunctionType
ALU = mybir.AluOpType

P = 128
K = 1024
UNIT = 512
NA = 4096
NB = 1024
GROUPS = NA // UNIT
FILL = 512
WARM = 4

FLOPS = 2 * NB * K * K + 2 * NA * NB * K


def tile_miscore_t_kernel(tc, y_a, y_b, W, b, out):
    nc = tc.nc
    with ExitStack() as ctx:
        ctx.enter_context(tc.manual_schedule())
        const = ctx.enter_context(tc.tile_pool(name="const", bufs=1))
        rawp = ctx.enter_context(tc.tile_pool(name="rawp", bufs=8))
        sortp = ctx.enter_context(tc.tile_pool(name="sortp", bufs=3))
        grpp = ctx.enter_context(tc.tile_pool(name="grpp", bufs=3))
        midp = ctx.enter_context(tc.tile_pool(name="midp", bufs=3))
        keep = ctx.enter_context(tc.tile_pool(name="keep", bufs=1))
        yacp = ctx.enter_context(tc.tile_pool(name="yacp", bufs=3))
        outp = ctx.enter_context(tc.tile_pool(name="outp", bufs=3))
        scrp = ctx.enter_context(tc.tile_pool(name="scrp", bufs=2))
        psum = ctx.enter_context(tc.psum_pool(name="psum", bufs=4))

        zl = const.tile([P, P], BF16, name="zl")
        zr = const.tile([P, UNIT], BF16, name="zr")
        nc.vector.memset(zl[:], 0.0)
        nc.vector.memset(zr[:], 0.0)
        ident = const.tile([P, P], F32, name="ident")
        make_identity(nc, ident[:])
        b_raw = const.tile([P, 8], BF16, name="b_raw")
        with nc.allow_non_contiguous_dma(reason="bias: 256 pieces of four elements, once"):
            nc.scalar.dma_start(
                out=b_raw[:].rearrange("p (a t) -> p a t", t=4),
                in_=b.rearrange("(a p t) -> p a t", p=P, t=4),
            )
        bias = const.tile([P, 8], F32, name="bias")
        warm = const.tile([P, 8], F32, name="warm")
        nc.vector.memset(warm[:, 0:1], 0.0)
        nc.scalar.activation(out=warm[:, 1:2], in_=warm[:, 0:1], func=ACT.Sigmoid)

        def idle_matmuls(n):
            for i in range(n):
                junk = psum.tile([P, UNIT], F32, name="junk", tag="mm")
                nc.tensor.matmul(out=junk[:], lhsT=zl[:], rhs=zr[:], start=True, stop=True)

        idle_matmuls(WARM)

        def rows_of(x):
            return x.rearrange("(g p r) k -> g p r k", p=P, r=4)

        def load(src, pieces):
            raw = rawp.tile([P, 4 * K], BF16, name="raw")
            n = 4 // pieces
            for i in range(pieces):
                nc.sync.dma_start(
                    out=raw[:, i * n * K : (i + 1) * n * K].rearrange("p (r k) -> p r k", k=K),
                    in_=src[:, i * n : (i + 1) * n, :],
                )
            return raw

        raw_yb = [None, None]
        raw_w = [None, None]
        raw_yb[0] = load(rows_of(y_b)[0], 2)
        raw_w[0] = load(rows_of(W)[0], 2)
        raw_w[1] = load(rows_of(W)[1], 2)
        raw_yb[1] = load(rows_of(y_b)[1], 2)

        def load_ya(g):
            return load(rows_of(y_a)[g], 1)

        raw_ya = [load_ya(g) for g in range(4)]

        def copy_on(which, dst, src):
            if which == "S":
                nc.scalar.copy(out=dst, in_=src)
            else:
                nc.vector.tensor_copy(out=dst, in_=src)

        def new_sorted():
            return sortp.tile([P, 4 * K], BF16, name="sorted")

        def sort_words(tile, raw, r0, r1, which="V"):
            cols = slice(r0 * K, r1 * K)
            copy_on(
                which,
                tile[:, cols].bitcast(F32).rearrange("p (a u i) -> p a u i", u=2, i=P),
                raw[:, cols].bitcast(F32).rearrange("p (a i u) -> p a u i", u=2, i=P),
            )

        def sorted_copy(raw, pieces=0):
            tile = new_sorted()
            if pieces == 0:
                sort_words(tile, raw, 0, 4)
            for i in range(pieces):
                cols = slice(i * 4 * K // pieces, (i + 1) * 4 * K // pieces)
                nc.gpsimd.tensor_copy(
                    out=tile[:, cols].bitcast(U32).rearrange("p (a u i) -> p a u i", u=2, i=P),
                    in_=raw[:, cols].bitcast(U32).rearrange("p (a i u) -> p a u i", u=2, i=P),
                )
            return tile

        def transpose_rows(tile, t, step=1):
            words = tile[:].bitcast(F32)
            xt = psum.tile([P, 4, P], F32, name="xt", tag="tp")
            for c in range(4):
                lo = t * (K // 2) + (c * P if step == 1 else (c // 2) * 2 * P + c % 2)
                nc.tensor.transpose(xt[:, c, :], words[:, lo : lo + step * (P - 1) + 1 : step], ident[:])
            return xt

        def new_grouped():
            return grpp.tile([P, 4 * K], BF16, name="grp", align_bytes=64)

        def evacuate(which, bank, grp, t):
            gw = grp[:].bitcast(F32).rearrange("p (g c u) -> p g c u", g=2, u=2)
            copy_on(
                which,
                gw[:, :, t * P : (t + 1) * P, :],
                bank[:].rearrange("p (g u) i -> p g i u", g=2),
            )

        def quantise(grp, op):
            nc.vector.quantize_mx(out=op[0][:].bitcast(FP8X4), scales=op[1][:], in_=grp[:])

        def transpose_unit(tile, engines, step=1, fill=False):
            grp = new_grouped()
            banks = []
            for t in range(4):
                banks.append(transpose_rows(tile, t, step))
                if fill and t % 2 == 1:
                    idle_matmuls(1)
            for t in range(4):
                evacuate(engines[t], banks[t], grp, t)
            return grp

        def operand(pool, name):
            codes = pool.tile([P, 2 * UNIT], U32, name=name + "_c", align_bytes=64)
            scales = pool.tile([P, 2 * UNIT], U8, name=name + "_s", align_bytes=64)
            return codes, scales

        def mx_group(acc, lc, ls, m0, rc, rs):
            for gk in range(2):
                ml = slice(gk * UNIT + m0, gk * UNIT + m0 + P)
                nl = slice(gk * UNIT, (gk + 1) * UNIT)
                nc.tensor.matmul_mx(
                    out=acc[:],
                    lhsT=lc[:, ml].bitcast(FP8X4),
                    lhsT_scale=ls[:, ml],
                    rhs=rc[:, nl].bitcast(FP8X4),
                    rhs_scale=rs[:, nl],
                    start=(gk == 0),
                    stop=(gk == 1),
                )

        yb_op = [operand(keep, "yb%d" % h) for h in range(2)]
        w_op = [operand(keep, "w%d" % g) for g in range(2)]
        pj_op = [operand(keep, "pj%d" % h) for h in range(2)]

        def project(go, h, engines="SSSS"):
            mid = midp.tile([P, 4 * UNIT], BF16, name="mid")
            for t in range(4):
                acc = psum.tile([P, UNIT], F32, name="acc", tag="mm")
                mx_group(acc, w_op[go][0], w_op[go][1], t * P, yb_op[h][0], yb_op[h][1])
                col = go * 4 + t
                dst = mid[:, t * UNIT : (t + 1) * UNIT]
                if engines[t] == "S":
                    nc.scalar.activation(
                        out=dst, in_=acc[:], func=ACT.Identity, bias=bias[:, col : col + 1], scale=1.0
                    )
                else:
                    nc.vector.tensor_scalar(
                        out=dst, in0=acc[:], scalar1=bias[:, col : col + 1], scalar2=None, op0=ALU.add
                    )
            return mid

        def regroup(mid):
            pgrp = midp.tile([P, 4 * UNIT], BF16, name="pgrp", align_bytes=64)
            nc.vector.tensor_copy(
                out=pgrp[:].rearrange("p (c i t) -> p c t i", i=4, t=4),
                in_=mid[:].rearrange("p (t c i) -> p c t i", t=4, i=4),
            )
            return pgrp

        def quantise_proj(go, h, pgrp):
            nl = slice(go * UNIT, (go + 1) * UNIT)
            nc.vector.quantize_mx(
                out=pj_op[h][0][:, nl].bitcast(FP8X4), scales=pj_op[h][1][:, nl], in_=pgrp[:]
            )

        out_v = out.rearrange("(g p r) (c k) -> g p r c k", p=P, r=4, k=FILL)

        def scores(g, op, sums, r, h):
            acc = psum.tile([P, UNIT], F32, name="acc", tag="mm")
            mx_group(acc, op[0], op[1], r * P, pj_op[h][0], pj_op[h][1])
            scr = scrp.tile([P, UNIT], F32, name="scr")
            col = 2 * r + h
            nc.scalar.activation(
                out=scr[:], in_=acc[:], func=ACT.Sigmoid, accum_out=sums[:, col : col + 1]
            )

        def finish(g, sums, ot, r):
            nc.vector.tensor_scalar(
                out=ot[:, r * FILL : (r + 1) * FILL],
                in0=sums[:, 2 * r : 2 * r + 1].to_broadcast([P, FILL]),
                scalar1=sums[:, 2 * r + 1 : 2 * r + 2],
                scalar2=1.0 / K,
                op0=ALU.add,
                op1=ALU.mult,
            )
            nc.sync.dma_start(
                out=out_v[g][:, r, :, :],
                in_=ot[:, r * FILL : (r + 1) * FILL].unsqueeze(1).to_broadcast([P, K // FILL, FILL]),
            )

        def sort_halves(raw):
            tile = new_sorted()
            sort_words(tile, raw, 0, 2)
            sort_words(tile, raw, 2, 4)
            return tile

        nc.vector.tensor_copy(out=bias[:], in_=b_raw[:])
        g_yb0 = transpose_unit(raw_yb[0], "SVSV", 2, True)
        g_w0 = transpose_unit(raw_w[0], "SSSS", 2, True)
        quantise(g_yb0, yb_op[0])
        quantise(g_w0, w_op[0])
        g_w1 = transpose_unit(raw_w[1], "SSVS", 2, True)
        s_yb1 = new_sorted()
        sort_words(s_yb1, raw_yb[1], 0, 2)
        mid00 = project(0, 0)
        quantise(g_w1, w_op[1])
        sort_words(s_yb1, raw_yb[1], 2, 4)
        g_yb1 = transpose_unit(s_yb1, "VSVS")
        raw_ya.append(load_ya(4))
        quantise(g_yb1, yb_op[1])
        p00 = regroup(mid00)
        mid10 = project(1, 0)
        quantise_proj(0, 0, p00)
        raw_ya.append(load_ya(5))
        g_ya = transpose_unit(raw_ya[0], "SVSV", 2)
        p10 = regroup(mid10)
        mid01 = project(0, 1)
        ya_op = operand(yacp, "ya")
        quantise(g_ya, ya_op)
        quantise_proj(1, 0, p10)
        p01 = regroup(mid01)
        mid11 = project(1, 1)
        raw_ya.append(load_ya(6))
        raw_ya.append(load_ya(7))
        late = None
        for g in range(GROUPS):
            sums = scrp.tile([P, 8], F32, name="sums", bufs=3)
            ot = outp.tile([P, 4 * FILL], F32, name="ot")
            more = g + 1 < GROUPS
            if more:
                next_op = operand(yacp, "ya")
                banks = [transpose_rows(raw_ya[1], t, 2) if g == 0 else transpose_rows(s_next, t) for t in range(4)]
                grp = new_grouped()
                if g == 0:
                    quantise_proj(0, 1, p01)
                    p11 = regroup(mid11)
                evacuate("V", banks[0], grp, 0)
                evacuate("S", banks[3], grp, 3)
                if g == 0:
                    quantise_proj(1, 1, p11)
            if late is not None:
                finish(*late)
            if more:
                for t in range(1, 3):
                    evacuate("V", banks[t], grp, t)
            if g == 0:
                for r in range(4):
                    scores(g, ya_op, sums, r, 0)
                s_next = sorted_copy(raw_ya[g + 2])
                for r in range(4):
                    scores(g, ya_op, sums, r, 1)
                    if r < 3:
                        finish(g, sums, ot, r)
                    if r == 0:
                        quantise(grp, next_op)
            else:
                if g + 2 < GROUPS:
                    s_next = sorted_copy(raw_ya[g + 2])
                for r in range(4):
                    for h in range(2):
                        scores(g, ya_op, sums, r, h)
                    if r < 3:
                        finish(g, sums, ot, r)
                    if r == 0 and more:
                        quantise(grp, next_op)
            late = (g, sums, ot, 3)
            if more:
                ya_op = next_op
        finish(*late)
